import numpy as np
import ml_dtypes


def mxq(x, axis, fmt="e4m3"):
    dtype, down = {"e4m3": (ml_dtypes.float8_e4m3fn, 7), "e5m2": (ml_dtypes.float8_e5m2, 14)}[fmt]
    v = np.moveaxis(np.asarray(x, np.float32).astype(ml_dtypes.bfloat16).astype(np.float64), axis, -1)
    blocks = v.reshape(v.shape[:-1] + (-1, 32))
    amax = np.abs(blocks).max(-1, keepdims=True)
    byte = np.maximum(np.where(amax > 0, np.frexp(amax)[1] - 1 + 127, 0) - down, 1)
    scale = np.exp2(byte - 127.0)
    codes = (blocks / scale).astype(np.float32).astype(dtype).astype(np.float64)
    return np.moveaxis((codes * scale).reshape(v.shape), -1, axis)


WIDE = False


def mx_kscale(k):
    if not WIDE:
        return np.ones(k)
    levels = np.array([10, -10, 5, -5, 0])
    a = np.random.permutation(np.resize(levels, k // 512 * 4)).reshape(k // 512, 4)
    idx = np.arange(k)
    return np.exp2(a[idx // 512, idx % 128 // 32])


BF16 = ml_dtypes.bfloat16


def bf(x):
    return np.asarray(x, np.float32).astype(BF16)


def f64(x):
    return np.asarray(x).astype(np.float64)


B, IN, H = 512, 1024, 1024


def hard_sigmoid(v):
    return np.clip(v / 6.0 + 0.5, 0.0, 1.0)


def hard_tanh(v):
    return np.clip(v, -1.0, 1.0)


def setup_inputs():
    s, t = mx_kscale(IN), mx_kscale(H)
    return {"input_": bf(np.random.standard_normal((B, IN)) * s),
            "h_0": bf(np.random.standard_normal((B, H)) * t),
            "c_0": bf(np.random.standard_normal((B, H))),
            "W_ih": bf(np.random.standard_normal((4 * H, IN)) * 1.25 / np.sqrt(IN) / s[None, :]),
            "W_hh": bf(np.random.standard_normal((4 * H, H)) * 1.25 / np.sqrt(H) / t[None, :]),
            "b_hh": bf(np.random.standard_normal(4 * H) * 0.3)}


def reference(input_, h_0, c_0, W_ih, W_hh, b_hh):
    wi = mxq(f64(input_), 1, "e4m3") @ mxq(f64(W_ih), 1, "e4m3").T
    wh_b = (mxq(f64(h_0), 1, "e4m3") @ mxq(f64(W_hh), 1, "e4m3").T) + f64(b_hh)
    h_x4 = wh_b + wi
    f, i, o, g = np.split(h_x4, 4, axis=1)
    new = hard_sigmoid(i) * hard_tanh(g)
    old = hard_sigmoid(f) * f64(c_0)
    c_1 = old + new
    h_1 = hard_sigmoid(o) * hard_tanh(c_1)
    return (h_1, c_1)

@@ -1,0 +1,224 @@
+from contextlib import ExitStack
+
+import concourse.mybir as mybir
+from concourse.masks import make_identity
+
+FLOPS = 2 * 512 * 4096 * 2048
+
+BF16 = mybir.dt.bfloat16
+F32 = mybir.dt.float32
+U32 = mybir.dt.uint32
+U8 = mybir.dt.uint8
+I32 = mybir.dt.int32
+FP8X4 = mybir.dt.float8_e4m3fn_x4
+ALU = mybir.AluOpType
+ACT = mybir.ActivationFunctionType
+
+P = 128
+CHUNKS = 8
+RAW_BUFS = 10
+STORE_GROUPS = ((0, 1), (2, 3), (4, 5), (6,), (7,))
+
+
+def tile_qlstmcell_kernel(tc, input_, h_0, c_0, W_ih, W_hh, b_hh, out_0, out_1):
+    nc = tc.nc
+    with ExitStack() as ctx:
+        ctx.enter_context(tc.manual_schedule())
+        const = ctx.enter_context(tc.tile_pool(name="const", bufs=1))
+        rawp = ctx.enter_context(tc.tile_pool(name="rawp", bufs=RAW_BUFS))
+        grp = ctx.enter_context(tc.tile_pool(name="grp", bufs=3))
+        wqp = ctx.enter_context(tc.tile_pool(name="wqp", bufs=4))
+        app = ctx.enter_context(tc.tile_pool(name="app", bufs=2))
+        tmp = ctx.enter_context(tc.tile_pool(name="tmp", bufs=1))
+        outp = ctx.enter_context(tc.tile_pool(name="outp", bufs=3))
+        trp = ctx.enter_context(tc.psum_pool(name="trp", bufs=4))
+        zp = ctx.enter_context(tc.psum_pool(name="zp", bufs=4))
+
+        ident = const.tile([P, P], F32, name="ident")
+        ones = const.tile([P, P], BF16, name="ones")
+        warm = const.tile([P, 8], F32, name="warm")
+        bz = const.tile([P, 4096], BF16, name="bz")
+        bt = const.tile([P, 4096], F32, name="bt")
+        c0 = const.tile([P, 4, 1024], BF16, name="c0")
+        acodes = [const.tile([P, 1024], U32, name="acodes%d" % m, align_bytes=64) for m in range(2)]
+        ascales = [const.tile([P, 1024], U8, name="ascales%d" % m, align_bytes=64) for m in range(2)]
+
+        w_views = [w.rearrange("(g c r) k -> c r g k", g=4, c=CHUNKS) for w in (W_ih, W_hh)]
+        o_views = [o.rearrange("(p j) h -> p j h", j=4) for o in (out_0, out_1)]
+
+        loads = [("x", input_.rearrange("(p j) k -> p j k", j=4)), ("w0", w_views[0][0]),
+                 ("h", h_0.rearrange("(p j) k -> p j k", j=4))]
+        for k in range(1, 2 * CHUNKS):
+            loads.append(("w%d" % k, w_views[k % 2][k // 2]))
+            if k == 3:
+                loads.append(("c0", c_0.rearrange("(p j) h -> p j h", j=4)))
+        raw = {}
+        state = {"issued": 0, "raw_live": 0}
+
+        def issue_loads():
+            while state["issued"] < len(loads):
+                key, view = loads[state["issued"]]
+                if key == "c0":
+                    nc.sync.dma_start(out=c0[:], in_=view)
+                else:
+                    if state["raw_live"] >= RAW_BUFS:
+                        return
+                    t = rawp.tile([P, 4096], BF16, name="raw_" + key, tag="raw")
+                    nc.sync.dma_start(out=t[:].rearrange("p (j k) -> p j k", j=4), in_=view)
+                    raw[key] = t
+                    state["raw_live"] += 1
+                state["issued"] += 1
+
+        grouped = {}
+        codes = {}
+
+        def transposes(key, vector_banks=()):
+            words = raw[key][:].bitcast(F32)
+            g_t = grp.tile([P, 4096], BF16, name="grouped_" + key, tag="grouped", align_bytes=64)
+            g32 = g_t[:].bitcast(F32)
+            grouped[key] = g_t
+            banks = []
+            for g in range(2):
+                for pair in range(2):
+                    bank = trp.tile([P, 512], F32, name="bank", tag="tr")
+                    for a in range(2):
+                        for u in range(2):
+                            col = (2 * pair + a) * 512 + 256 * g + 128 * u
+                            nc.tensor.transpose(bank[:, (2 * a + u) * P:(2 * a + u + 1) * P],
+                                                words[:, col:col + P], ident[:])
+                    banks.append(bank)
+            for q in range(4):
+                dst = g32[:, q * 512:(q + 1) * 512].rearrange("p (a r u) -> p a r u", a=2, u=2)
+                src = banks[q][:].rearrange("p (a u r) -> p a r u", a=2, u=2)
+                if q in vector_banks:
+                    nc.vector.tensor_copy(out=dst, in_=src)
+                else:
+                    nc.scalar.copy(out=dst, in_=src)
+            state["raw_live"] -= 1
+            issue_loads()
+
+        def quantise(key):
+            if key == "x" or key == "h":
+                m = 0 if key == "x" else 1
+                cd, sc = acodes[m], ascales[m]
+            else:
+                cd = wqp.tile([P, 1024], U32, name="wcodes", tag="wcodes", align_bytes=64)
+                sc = wqp.tile([P, 1024], U8, name="wscales", tag="wscales", align_bytes=64)
+            nc.vector.quantize_mx(out=cd[:].bitcast(FP8X4), scales=sc[:], in_=grouped[key][:])
+            codes[key] = (cd, sc)
+
+        zbanks = {}
+
+        def mx(k):
+            c, m = k // 2, k % 2
+            if m == 0:
+                zbanks[c] = [zp.tile([P, 512], F32, name="z%d" % bb, tag="z") for bb in range(4)]
+            cd, sc = codes["w%d" % k]
+            for bb in range(4):
+                for g in range(2):
+                    a0 = g * 512 + bb * P
+                    nc.tensor.matmul_mx(out=zbanks[c][bb][:],
+                                        lhsT=acodes[m][:, a0:a0 + P].bitcast(FP8X4),
+                                        lhsT_scale=ascales[m][:, a0:a0 + P],
+                                        rhs=cd[:, g * 512:(g + 1) * 512].bitcast(FP8X4),
+                                        rhs_scale=sc[:, g * 512:(g + 1) * 512],
+                                        start=(m == 0 and g == 0), stop=(m == 1 and g == 1))
+
+        def bias_rows(first, last):
+            btv = bt[:].rearrange("p (c g r) -> p c g r", c=CHUNKS, g=4)
+            for i in range(first, last):
+                gate, half = i // 2, i % 2
+                ps = zp.tile([P, 512], F32, name="bias_ps", tag="z")
+                nc.tensor.matmul(ps[:], lhsT=ones[:], rhs=bz[:, i * 512:(i + 1) * 512], start=True, stop=True)
+                nc.vector.tensor_scalar(out=btv[:, half * 4:(half + 1) * 4, gate, :],
+                                        in0=ps[:].rearrange("p (c r) -> p c r", c=4),
+                                        scalar1=(1.0 if gate == 3 else 3.0), scalar2=None, op0=ALU.add)
+
+        acts = {}
+
+        def bias_add(c):
+            a_t = app.tile([P, 4, 512], F32, name="a_t", tag="a")
+            acts[c] = a_t
+            for bb in range(4):
+                nc.vector.tensor_tensor(out=a_t[:, bb, :], in0=zbanks[c][bb][:],
+                                        in1=bt[:, c * 512:(c + 1) * 512], op=ALU.add)
+
+        def relu(c, b0, b1):
+            a_t = acts[c]
+            nc.scalar.activation(out=a_t[:, b0:b1, 0:384], in_=a_t[:, b0:b1, 0:384], func=ACT.Relu, scale=1.0 / 6.0)
+            nc.scalar.activation(out=a_t[:, b0:b1, 384:512], in_=a_t[:, b0:b1, 384:512], func=ACT.Relu)
+
+        outs = {}
+
+        def gates(c, b0, b1):
+            a_t = acts[c]
+            group = [gr for gr in STORE_GROUPS if c in gr][0]
+            width = P * len(group)
+            if c == group[0] and b0 == 0:
+                outs[group] = (outp.tile([P, 4, width], F32, name="h1_t", tag="h1_%d" % width),
+                               outp.tile([P, 4, width], F32, name="c1_t", tag="c1_%d" % width))
+            h1_t, c1_t = outs[group]
+            lo = (c - group[0]) * P
+            old = tmp.tile([P, 4, P], F32, name="old")
+            new = tmp.tile([P, 4, P], F32, name="new")
+            gcl = tmp.tile([P, 4, P], F32, name="gcl")
+            tcl = tmp.tile([P, 4, P], F32, name="tcl")
+            nc.vector.scalar_tensor_tensor(out=old[:, b0:b1, :], in0=a_t[:, b0:b1, 0:128], scalar=1.0,
+                                           in1=c0[:, b0:b1, c * P:(c + 1) * P], op0=ALU.min, op1=ALU.mult)
+            nc.vector.tensor_scalar(out=gcl[:, b0:b1, :], in0=a_t[:, b0:b1, 384:512], scalar1=2.0, scalar2=-1.0,
+                                    op0=ALU.min, op1=ALU.add)
+            nc.vector.scalar_tensor_tensor(out=new[:, b0:b1, :], in0=a_t[:, b0:b1, 128:256], scalar=1.0,
+                                           in1=gcl[:, b0:b1, :], op0=ALU.min, op1=ALU.mult)
+            nc.vector.tensor_tensor(out=c1_t[:, b0:b1, lo:lo + P], in0=old[:, b0:b1, :], in1=new[:, b0:b1, :],
+                                    op=ALU.add)
+            nc.vector.tensor_scalar(out=tcl[:, b0:b1, :], in0=c1_t[:, b0:b1, lo:lo + P], scalar1=-1.0, scalar2=1.0,
+                                    op0=ALU.max, op1=ALU.min)
+            nc.vector.scalar_tensor_tensor(out=h1_t[:, b0:b1, lo:lo + P], in0=a_t[:, b0:b1, 256:384], scalar=1.0,
+                                           in1=tcl[:, b0:b1, :], op0=ALU.min, op1=ALU.mult)
+            if c == group[-1]:
+                col = group[0] * P
+                nc.sync.dma_start(out=o_views[1][:, b0:b1, col:col + width], in_=c1_t[:, b0:b1, :])
+                nc.sync.dma_start(out=o_views[0][:, b0:b1, col:col + width], in_=h1_t[:, b0:b1, :])
+
+        nc.vector.memset(bz[:].bitcast(I32), 0)
+        nc.vector.memset(ones[:], 1.0)
+        nc.vector.memset(warm[:], 0.0)
+        make_identity(nc, ident[:])
+        nc.scalar.dma_start(out=bz[0:1, :], in_=b_hh.rearrange("(o n) -> o n", o=1))
+        nc.scalar.activation(out=warm[:], in_=warm[:], func=ACT.Relu)
+        issue_loads()
+
+        bias_rows(0, 4)
+        transposes("x")
+        bias_rows(4, 8)
+        transposes("w0")
+        quantise("x")
+        transposes("h")
+        quantise("w0")
+        mx(0)
+        transposes("w1")
+        quantise("h")
+        transposes("w2")
+        quantise("w1")
+        transposes("w3")
+        quantise("w2")
+        mx(1)
+        bias_add(0)
+        for c in range(1, CHUNKS):
+            relu(c - 1, 0, 2)
+            relu(c - 1, 2, 4)
+            if 2 * c + 2 < 2 * CHUNKS:
+                transposes("w%d" % (2 * c + 2))
+            quantise("w%d" % (2 * c + 1))
+            mx(2 * c)
+            gates(c - 1, 0, 4)
+            if 2 * c + 3 < 2 * CHUNKS:
+                transposes("w%d" % (2 * c + 3))
+                quantise("w%d" % (2 * c + 2))
+            mx(2 * c + 1)
+            bias_add(c)
+        last = CHUNKS - 1
+        relu(last, 0, 2)
+        relu(last, 2, 4)
+        gates(last, 0, 2)
+        gates(last, 2, 4)

@@ -18,6 +18,7 @@ P = 128
 CHUNKS = 8
 RAW_BUFS = 10
 STORE_GROUPS = ((0, 1), (2, 3), (4, 5), (6,), (7,))
+GPSIMD_HELPS = True
 
 
 def tile_qlstmcell_kernel(tc, input_, h_0, c_0, W_ih, W_hh, b_hh, out_0, out_1):
@@ -29,7 +30,7 @@ def tile_qlstmcell_kernel(tc, input_, h_0, c_0, W_ih, W_hh, b_hh, out_0, out_1):
         grp = ctx.enter_context(tc.tile_pool(name="grp", bufs=3))
         wqp = ctx.enter_context(tc.tile_pool(name="wqp", bufs=4))
         app = ctx.enter_context(tc.tile_pool(name="app", bufs=2))
-        tmp = ctx.enter_context(tc.tile_pool(name="tmp", bufs=1))
+        tmp = ctx.enter_context(tc.tile_pool(name="tmp", bufs=2))
         outp = ctx.enter_context(tc.tile_pool(name="outp", bufs=3))
         trp = ctx.enter_context(tc.psum_pool(name="trp", bufs=4))
         zp = ctx.enter_context(tc.psum_pool(name="zp", bufs=4))
@@ -38,7 +39,7 @@ def tile_qlstmcell_kernel(tc, input_, h_0, c_0, W_ih, W_hh, b_hh, out_0, out_1):
         ones = const.tile([P, P], BF16, name="ones")
         warm = const.tile([P, 8], F32, name="warm")
         bz = const.tile([P, 4096], BF16, name="bz")
-        bt = const.tile([P, 4096], F32, name="bt")
+        bt = const.tile([P, 4096], BF16, name="bt")
         c0 = const.tile([P, 4, 1024], BF16, name="c0")
         acodes = [const.tile([P, 1024], U32, name="acodes%d" % m, align_bytes=64) for m in range(2)]
         ascales = [const.tile([P, 1024], U8, name="ascales%d" % m, align_bytes=64) for m in range(2)]
@@ -46,11 +47,11 @@ def tile_qlstmcell_kernel(tc, input_, h_0, c_0, W_ih, W_hh, b_hh, out_0, out_1):
         w_views = [w.rearrange("(g c r) k -> c r g k", g=4, c=CHUNKS) for w in (W_ih, W_hh)]
         o_views = [o.rearrange("(p j) h -> p j h", j=4) for o in (out_0, out_1)]
 
-        loads = [("x", input_.rearrange("(p j) k -> p j k", j=4)), ("w0", w_views[0][0]),
-                 ("h", h_0.rearrange("(p j) k -> p j k", j=4))]
+        loads = [("x", input_.rearrange("(p j) k -> p j k", j=4)), ("b", b_hh.rearrange("(o n) -> o n", o=1)),
+                 ("w0", w_views[0][0]), ("h", h_0.rearrange("(p j) k -> p j k", j=4))]
         for k in range(1, 2 * CHUNKS):
             loads.append(("w%d" % k, w_views[k % 2][k // 2]))
-            if k == 3:
+            if k == 4:
                 loads.append(("c0", c_0.rearrange("(p j) h -> p j h", j=4)))
         raw = {}
         state = {"issued": 0, "raw_live": 0}
@@ -60,6 +61,8 @@ def tile_qlstmcell_kernel(tc, input_, h_0, c_0, W_ih, W_hh, b_hh, out_0, out_1):
                 key, view = loads[state["issued"]]
                 if key == "c0":
                     nc.sync.dma_start(out=c0[:], in_=view)
+                elif key == "b":
+                    nc.sync.dma_start(out=bz[0:1, :], in_=view)
                 else:
                     if state["raw_live"] >= RAW_BUFS:
                         return
@@ -109,48 +112,45 @@ def tile_qlstmcell_kernel(tc, input_, h_0, c_0, W_ih, W_hh, b_hh, out_0, out_1):
 
         zbanks = {}
 
-        def mx(k):
-            c, m = k // 2, k % 2
-            if m == 0:
-                zbanks[c] = [zp.tile([P, 512], F32, name="z%d" % bb, tag="z") for bb in range(4)]
-            cd, sc = codes["w%d" % k]
-            for bb in range(4):
-                for g in range(2):
-                    a0 = g * 512 + bb * P
-                    nc.tensor.matmul_mx(out=zbanks[c][bb][:],
-                                        lhsT=acodes[m][:, a0:a0 + P].bitcast(FP8X4),
-                                        lhsT_scale=ascales[m][:, a0:a0 + P],
-                                        rhs=cd[:, g * 512:(g + 1) * 512].bitcast(FP8X4),
-                                        rhs_scale=sc[:, g * 512:(g + 1) * 512],
-                                        start=(m == 0 and g == 0), stop=(m == 1 and g == 1))
+        def open_banks(c):
+            zbanks[c] = [zp.tile([P, 512], F32, name="z%d" % bb, tag="z") for bb in range(4)]
 
-        def bias_rows(first, last):
-            btv = bt[:].rearrange("p (c g r) -> p c g r", c=CHUNKS, g=4)
-            for i in range(first, last):
-                gate, half = i // 2, i % 2
-                ps = zp.tile([P, 512], F32, name="bias_ps", tag="z")
-                nc.tensor.matmul(ps[:], lhsT=ones[:], rhs=bz[:, i * 512:(i + 1) * 512], start=True, stop=True)
-                nc.vector.tensor_scalar(out=btv[:, half * 4:(half + 1) * 4, gate, :],
-                                        in0=ps[:].rearrange("p (c r) -> p c r", c=4),
-                                        scalar1=(1.0 if gate == 3 else 3.0), scalar2=None, op0=ALU.add)
+        def mx_passes(c, bb, m):
+            cd, sc = codes["w%d" % (2 * c + m)]
+            for g in range(2):
+                a0 = g * 512 + bb * P
+                nc.tensor.matmul_mx(out=zbanks[c][bb][:],
+                                    lhsT=acodes[m][:, a0:a0 + P].bitcast(FP8X4),
+                                    lhsT_scale=ascales[m][:, a0:a0 + P],
+                                    rhs=cd[:, g * 512:(g + 1) * 512].bitcast(FP8X4),
+                                    rhs_scale=sc[:, g * 512:(g + 1) * 512],
+                                    start=(m == 0 and g == 0), stop=(m == 1 and g == 1))
+
+        def bias_rows(gate):
+            ps = zp.tile([P, 1024], BF16, name="bias_ps", tag="z")
+            for half in range(2):
+                nc.tensor.matmul(ps[:, half * 512:(half + 1) * 512], lhsT=ones[:],
+                                 rhs=bz[:, gate * 1024 + half * 512:gate * 1024 + (half + 1) * 512],
+                                 start=True, stop=True)
+            nc.vector.tensor_copy(out=bt[:].rearrange("p (c g r) -> p c g r", c=CHUNKS, g=4)[:, :, gate, :],
+                                  in_=ps[:].rearrange("p (c r) -> p c r", c=CHUNKS))
 
         acts = {}
 
-        def bias_add(c):
-            a_t = app.tile([P, 4, 512], F32, name="a_t", tag="a")
-            acts[c] = a_t
-            for bb in range(4):
-                nc.vector.tensor_tensor(out=a_t[:, bb, :], in0=zbanks[c][bb][:],
-                                        in1=bt[:, c * 512:(c + 1) * 512], op=ALU.add)
+        def bias_add(c, bb):
+            if bb == 0:
+                acts[c] = app.tile([P, 4, 512], F32, name="a_t", tag="a")
+            nc.vector.tensor_tensor(out=acts[c][:, bb, :], in0=zbanks[c][bb][:],
+                                    in1=bt[:, c * 512:(c + 1) * 512], op=ALU.add)
 
         def relu(c, b0, b1):
             a_t = acts[c]
-            nc.scalar.activation(out=a_t[:, b0:b1, 0:384], in_=a_t[:, b0:b1, 0:384], func=ACT.Relu, scale=1.0 / 6.0)
-            nc.scalar.activation(out=a_t[:, b0:b1, 384:512], in_=a_t[:, b0:b1, 384:512], func=ACT.Relu)
+            nc.scalar.activation(out=a_t[:, b0:b1, 0:384], in_=a_t[:, b0:b1, 0:384], func=ACT.Relu,
+                                 bias=0.5, scale=1.0 / 6.0)
 
         outs = {}
 
-        def gates(c, b0, b1):
+        def gate_chain(c, b0, b1):
             a_t = acts[c]
             group = [gr for gr in STORE_GROUPS if c in gr][0]
             width = P * len(group)
@@ -159,66 +159,103 @@ def tile_qlstmcell_kernel(tc, input_, h_0, c_0, W_ih, W_hh, b_hh, out_0, out_1):
                                outp.tile([P, 4, width], F32, name="c1_t", tag="c1_%d" % width))
             h1_t, c1_t = outs[group]
             lo = (c - group[0]) * P
+            col = group[0] * P
             old = tmp.tile([P, 4, P], F32, name="old")
             new = tmp.tile([P, 4, P], F32, name="new")
             gcl = tmp.tile([P, 4, P], F32, name="gcl")
             tcl = tmp.tile([P, 4, P], F32, name="tcl")
-            nc.vector.scalar_tensor_tensor(out=old[:, b0:b1, :], in0=a_t[:, b0:b1, 0:128], scalar=1.0,
-                                           in1=c0[:, b0:b1, c * P:(c + 1) * P], op0=ALU.min, op1=ALU.mult)
-            nc.vector.tensor_scalar(out=gcl[:, b0:b1, :], in0=a_t[:, b0:b1, 384:512], scalar1=2.0, scalar2=-1.0,
-                                    op0=ALU.min, op1=ALU.add)
-            nc.vector.scalar_tensor_tensor(out=new[:, b0:b1, :], in0=a_t[:, b0:b1, 128:256], scalar=1.0,
-                                           in1=gcl[:, b0:b1, :], op0=ALU.min, op1=ALU.mult)
-            nc.vector.tensor_tensor(out=c1_t[:, b0:b1, lo:lo + P], in0=old[:, b0:b1, :], in1=new[:, b0:b1, :],
-                                    op=ALU.add)
-            nc.vector.tensor_scalar(out=tcl[:, b0:b1, :], in0=c1_t[:, b0:b1, lo:lo + P], scalar1=-1.0, scalar2=1.0,
-                                    op0=ALU.max, op1=ALU.min)
-            nc.vector.scalar_tensor_tensor(out=h1_t[:, b0:b1, lo:lo + P], in0=a_t[:, b0:b1, 256:384], scalar=1.0,
-                                           in1=tcl[:, b0:b1, :], op0=ALU.min, op1=ALU.mult)
-            if c == group[-1]:
-                col = group[0] * P
-                nc.sync.dma_start(out=o_views[1][:, b0:b1, col:col + width], in_=c1_t[:, b0:b1, :])
-                nc.sync.dma_start(out=o_views[0][:, b0:b1, col:col + width], in_=h1_t[:, b0:b1, :])
+            helper = nc.gpsimd if (GPSIMD_HELPS and c + 1 < CHUNKS) else nc.vector
+
+            def s_gcl():
+                nc.vector.tensor_scalar(out=gcl[:, b0:b1, :], in0=a_t[:, b0:b1, 384:512], scalar1=-1.0, scalar2=1.0,
+                                        op0=ALU.max, op1=ALU.min)
+
+            def s_old():
+                nc.vector.scalar_tensor_tensor(out=old[:, b0:b1, :], in0=a_t[:, b0:b1, 0:128], scalar=1.0,
+                                               in1=c0[:, b0:b1, c * P:(c + 1) * P], op0=ALU.min, op1=ALU.mult)
+
+            def s_new():
+                nc.vector.scalar_tensor_tensor(out=new[:, b0:b1, :], in0=a_t[:, b0:b1, 128:256], scalar=1.0,
+                                               in1=gcl[:, b0:b1, :], op0=ALU.min, op1=ALU.mult)
+
+            def s_c1():
+                helper.tensor_tensor(out=c1_t[:, b0:b1, lo:lo + P], in0=old[:, b0:b1, :], in1=new[:, b0:b1, :],
+                                     op=ALU.add)
+                if c == group[-1]:
+                    nc.sync.dma_start(out=o_views[1][:, b0:b1, col:col + width], in_=c1_t[:, b0:b1, :])
+
+            def s_tcl():
+                helper.tensor_scalar(out=tcl[:, b0:b1, :], in0=c1_t[:, b0:b1, lo:lo + P], scalar1=-1.0, scalar2=1.0,
+                                     op0=ALU.max, op1=ALU.min)
+
+            def s_h1():
+                nc.vector.scalar_tensor_tensor(out=h1_t[:, b0:b1, lo:lo + P], in0=a_t[:, b0:b1, 256:384], scalar=1.0,
+                                               in1=tcl[:, b0:b1, :], op0=ALU.min, op1=ALU.mult)
+                if c == group[-1]:
+                    nc.sync.dma_start(out=o_views[0][:, b0:b1, col:col + width], in_=h1_t[:, b0:b1, :])
+
+            return [s_gcl, s_old, s_new, s_c1, s_tcl, s_h1]
+
+        def alternate(first, second):
+            for i in range(max(len(first), len(second))):
+                for calls in (first, second):
+                    if i < len(calls):
+                        calls[i]()
 
         nc.vector.memset(bz[:].bitcast(I32), 0)
         nc.vector.memset(ones[:], 1.0)
         nc.vector.memset(warm[:], 0.0)
         make_identity(nc, ident[:])
-        nc.scalar.dma_start(out=bz[0:1, :], in_=b_hh.rearrange("(o n) -> o n", o=1))
-        nc.scalar.activation(out=warm[:], in_=warm[:], func=ACT.Relu)
+        nc.scalar.activation(out=warm[:], in_=warm[:], func=ACT.Relu, bias=0.5, scale=1.0 / 6.0)
         issue_loads()
 
-        bias_rows(0, 4)
         transposes("x")
-        bias_rows(4, 8)
+        bias_rows(0)
+        bias_rows(1)
         transposes("w0")
         quantise("x")
+        bias_rows(2)
+        bias_rows(3)
         transposes("h")
         quantise("w0")
-        mx(0)
+        open_banks(0)
+        for bb in range(4):
+            mx_passes(0, bb, 0)
         transposes("w1")
         quantise("h")
         transposes("w2")
         quantise("w1")
         transposes("w3")
         quantise("w2")
-        mx(1)
-        bias_add(0)
+        for bb in range(4):
+            mx_passes(0, bb, 1)
+        for bb in range(4):
+            bias_add(0, bb)
         for c in range(1, CHUNKS):
             relu(c - 1, 0, 2)
             relu(c - 1, 2, 4)
-            if 2 * c + 2 < 2 * CHUNKS:
+            chain = gate_chain(c - 1, 0, 4)
+            if c + 1 < CHUNKS:
                 transposes("w%d" % (2 * c + 2))
             quantise("w%d" % (2 * c + 1))
-            mx(2 * c)
-            gates(c - 1, 0, 4)
-            if 2 * c + 3 < 2 * CHUNKS:
+            open_banks(c)
+            for bb in range(4):
+                mx_passes(c, bb, 0)
+            for call in chain[0:3]:
+                call()
+            if c + 1 < CHUNKS:
                 transposes("w%d" % (2 * c + 3))
                 quantise("w%d" % (2 * c + 2))
-            mx(2 * c + 1)
-            bias_add(c)
+            for bb in range(4):
+                mx_passes(c, bb, 1)
+            adds = [lambda bb=bb: bias_add(c, bb) for bb in range(4)]
+            if GPSIMD_HELPS:
+                alternate(chain[3:5], [])
+                alternate(adds, [])
+                chain[5]()
+            else:
+                alternate(chain[3:6], adds)
         last = CHUNKS - 1
         relu(last, 0, 2)
         relu(last, 2, 4)
-        gates(last, 0, 2)
-        gates(last, 2, 4)
+        alternate(gate_chain(last, 0, 2), gate_chain(last, 2, 4))

@@ -18,7 +18,7 @@ P = 128
 CHUNKS = 8
 RAW_BUFS = 10
 STORE_GROUPS = ((0, 1), (2, 3), (4, 5), (6,), (7,))
-GPSIMD_HELPS = True
+GPSIMD_HELPS = False
 
 
 def tile_qlstmcell_kernel(tc, input_, h_0, c_0, W_ih, W_hh, b_hh, out_0, out_1):

@@ -218,10 +218,10 @@ def tile_qlstmcell_kernel(tc, input_, h_0, c_0, W_ih, W_hh, b_hh, out_0, out_1):
         bias_rows(3)
         transposes("h")
         quantise("w0")
+        transposes("w1")
         open_banks(0)
         for bb in range(4):
             mx_passes(0, bb, 0)
-        transposes("w1")
         quantise("h")
         transposes("w2")
         quantise("w1")
@@ -232,11 +232,11 @@ def tile_qlstmcell_kernel(tc, input_, h_0, c_0, W_ih, W_hh, b_hh, out_0, out_1):
         for bb in range(4):
             bias_add(0, bb)
         for c in range(1, CHUNKS):
+            if c + 1 < CHUNKS:
+                transposes("w%d" % (2 * c + 2))
             relu(c - 1, 0, 2)
             relu(c - 1, 2, 4)
             chain = gate_chain(c - 1, 0, 4)
-            if c + 1 < CHUNKS:
-                transposes("w%d" % (2 * c + 2))
             quantise("w%d" % (2 * c + 1))
             open_banks(c)
             for bb in range(4):

@@ -164,10 +164,10 @@ def tile_qlstmcell_kernel(tc, input_, h_0, c_0, W_ih, W_hh, b_hh, out_0, out_1):
             new = tmp.tile([P, 4, P], F32, name="new")
             gcl = tmp.tile([P, 4, P], F32, name="gcl")
             tcl = tmp.tile([P, 4, P], F32, name="tcl")
-            helper = nc.gpsimd if (GPSIMD_HELPS and c + 1 < CHUNKS) else nc.vector
+            clipper = nc.gpsimd if c + 1 < CHUNKS else nc.vector
 
             def s_gcl():
-                nc.vector.tensor_scalar(out=gcl[:, b0:b1, :], in0=a_t[:, b0:b1, 384:512], scalar1=-1.0, scalar2=1.0,
+                clipper.tensor_scalar(out=gcl[:, b0:b1, :], in0=a_t[:, b0:b1, 384:512], scalar1=-1.0, scalar2=1.0,
                                         op0=ALU.max, op1=ALU.min)
 
             def s_old():
@@ -179,13 +179,13 @@ def tile_qlstmcell_kernel(tc, input_, h_0, c_0, W_ih, W_hh, b_hh, out_0, out_1):
                                                in1=gcl[:, b0:b1, :], op0=ALU.min, op1=ALU.mult)
 
             def s_c1():
-                helper.tensor_tensor(out=c1_t[:, b0:b1, lo:lo + P], in0=old[:, b0:b1, :], in1=new[:, b0:b1, :],
+                nc.vector.tensor_tensor(out=c1_t[:, b0:b1, lo:lo + P], in0=old[:, b0:b1, :], in1=new[:, b0:b1, :],
                                      op=ALU.add)
                 if c == group[-1]:
                     nc.sync.dma_start(out=o_views[1][:, b0:b1, col:col + width], in_=c1_t[:, b0:b1, :])
 
             def s_tcl():
-                helper.tensor_scalar(out=tcl[:, b0:b1, :], in0=c1_t[:, b0:b1, lo:lo + P], scalar1=-1.0, scalar2=1.0,
+                clipper.tensor_scalar(out=tcl[:, b0:b1, :], in0=c1_t[:, b0:b1, lo:lo + P], scalar1=-1.0, scalar2=1.0,
                                      op0=ALU.max, op1=ALU.min)
 
             def s_h1():

@@ -15,10 +15,12 @@ ALU = mybir.AluOpType
 ACT = mybir.ActivationFunctionType
 
 P = 128
+SLABS = 4
+K = 1024
+BANK = 512
 CHUNKS = 8
 RAW_BUFS = 10
 STORE_GROUPS = ((0, 1), (2, 3), (4, 5), (6,), (7,))
-GPSIMD_HELPS = False
 
 
 def tile_qlstmcell_kernel(tc, input_, h_0, c_0, W_ih, W_hh, b_hh, out_0, out_1):
@@ -26,183 +28,173 @@ def tile_qlstmcell_kernel(tc, input_, h_0, c_0, W_ih, W_hh, b_hh, out_0, out_1):
     with ExitStack() as ctx:
         ctx.enter_context(tc.manual_schedule())
         const = ctx.enter_context(tc.tile_pool(name="const", bufs=1))
-        rawp = ctx.enter_context(tc.tile_pool(name="rawp", bufs=RAW_BUFS))
-        grp = ctx.enter_context(tc.tile_pool(name="grp", bufs=3))
-        wqp = ctx.enter_context(tc.tile_pool(name="wqp", bufs=4))
-        app = ctx.enter_context(tc.tile_pool(name="app", bufs=2))
-        tmp = ctx.enter_context(tc.tile_pool(name="tmp", bufs=2))
-        outp = ctx.enter_context(tc.tile_pool(name="outp", bufs=3))
-        trp = ctx.enter_context(tc.psum_pool(name="trp", bufs=4))
-        zp = ctx.enter_context(tc.psum_pool(name="zp", bufs=4))
+        raw_pool = ctx.enter_context(tc.tile_pool(name="raw_pool", bufs=RAW_BUFS))
+        grouped_pool = ctx.enter_context(tc.tile_pool(name="grouped_pool", bufs=3))
+        weight_pool = ctx.enter_context(tc.tile_pool(name="weight_pool", bufs=4))
+        sums_pool = ctx.enter_context(tc.tile_pool(name="sums_pool", bufs=2))
+        gate_pool = ctx.enter_context(tc.tile_pool(name="gate_pool", bufs=2))
+        out_pool = ctx.enter_context(tc.tile_pool(name="out_pool", bufs=3))
+        tr_pool = ctx.enter_context(tc.psum_pool(name="tr_pool", bufs=4))
+        z_pool = ctx.enter_context(tc.psum_pool(name="z_pool", bufs=4))
 
         ident = const.tile([P, P], F32, name="ident")
         ones = const.tile([P, P], BF16, name="ones")
         warm = const.tile([P, 8], F32, name="warm")
-        bz = const.tile([P, 4096], BF16, name="bz")
-        bt = const.tile([P, 4096], BF16, name="bt")
-        c0 = const.tile([P, 4, 1024], BF16, name="c0")
-        acodes = [const.tile([P, 1024], U32, name="acodes%d" % m, align_bytes=64) for m in range(2)]
-        ascales = [const.tile([P, 1024], U8, name="ascales%d" % m, align_bytes=64) for m in range(2)]
+        bias_row = const.tile([P, SLABS * K], BF16, name="bias_row")
+        bias_all = const.tile([P, CHUNKS * BANK], BF16, name="bias_all")
+        c0_sb = const.tile([P, SLABS, K], BF16, name="c0_sb")
+        act_codes = [const.tile([P, 2 * BANK], U32, name="act_codes%d" % m, align_bytes=64) for m in range(2)]
+        act_scales = [const.tile([P, 2 * BANK], U8, name="act_scales%d" % m, align_bytes=64) for m in range(2)]
 
-        w_views = [w.rearrange("(g c r) k -> c r g k", g=4, c=CHUNKS) for w in (W_ih, W_hh)]
-        o_views = [o.rearrange("(p j) h -> p j h", j=4) for o in (out_0, out_1)]
+        weight_views = [w.rearrange("(g c r) k -> c r g k", g=SLABS, c=CHUNKS) for w in (W_ih, W_hh)]
+        out_views = [o.rearrange("(p j) h -> p j h", j=SLABS) for o in (out_0, out_1)]
 
-        loads = [("x", input_.rearrange("(p j) k -> p j k", j=4)), ("b", b_hh.rearrange("(o n) -> o n", o=1)),
-                 ("w0", w_views[0][0]), ("h", h_0.rearrange("(p j) k -> p j k", j=4))]
-        for k in range(1, 2 * CHUNKS):
-            loads.append(("w%d" % k, w_views[k % 2][k // 2]))
-            if k == 4:
-                loads.append(("c0", c_0.rearrange("(p j) h -> p j h", j=4)))
+        loads = [("x", input_.rearrange("(p j) k -> p j k", j=SLABS)),
+                 ("bias", b_hh.rearrange("(o n) -> o n", o=1)),
+                 ("w0", weight_views[0][0]),
+                 ("h", h_0.rearrange("(p j) k -> p j k", j=SLABS))]
+        for t in range(1, 2 * CHUNKS):
+            loads.append(("w%d" % t, weight_views[t % 2][t // 2]))
+            if t == 4:
+                loads.append(("c0", c_0.rearrange("(p j) h -> p j h", j=SLABS)))
         raw = {}
-        state = {"issued": 0, "raw_live": 0}
+        progress = {"issued": 0, "waiting": 0}
 
         def issue_loads():
-            while state["issued"] < len(loads):
-                key, view = loads[state["issued"]]
+            while progress["issued"] < len(loads):
+                key, view = loads[progress["issued"]]
                 if key == "c0":
-                    nc.sync.dma_start(out=c0[:], in_=view)
-                elif key == "b":
-                    nc.sync.dma_start(out=bz[0:1, :], in_=view)
+                    nc.sync.dma_start(out=c0_sb[:], in_=view)
+                elif key == "bias":
+                    nc.sync.dma_start(out=bias_row[0:1, :], in_=view)
                 else:
-                    if state["raw_live"] >= RAW_BUFS:
+                    if progress["waiting"] == RAW_BUFS:
                         return
-                    t = rawp.tile([P, 4096], BF16, name="raw_" + key, tag="raw")
-                    nc.sync.dma_start(out=t[:].rearrange("p (j k) -> p j k", j=4), in_=view)
-                    raw[key] = t
-                    state["raw_live"] += 1
-                state["issued"] += 1
+                    raw[key] = raw_pool.tile([P, SLABS * K], BF16, name="raw_" + key, tag="raw")
+                    nc.sync.dma_start(out=raw[key][:].rearrange("p (j k) -> p j k", j=SLABS), in_=view)
+                    progress["waiting"] += 1
+                progress["issued"] += 1
 
         grouped = {}
         codes = {}
 
-        def transposes(key, vector_banks=()):
+        def transposes(key):
             words = raw[key][:].bitcast(F32)
-            g_t = grp.tile([P, 4096], BF16, name="grouped_" + key, tag="grouped", align_bytes=64)
-            g32 = g_t[:].bitcast(F32)
-            grouped[key] = g_t
+            grouped[key] = grouped_pool.tile([P, 8 * BANK], BF16, name="grouped_" + key, tag="grouped",
+                                             align_bytes=64)
+            grouped_words = grouped[key][:].bitcast(F32)
             banks = []
-            for g in range(2):
-                for pair in range(2):
-                    bank = trp.tile([P, 512], F32, name="bank", tag="tr")
+            for s in range(2):
+                for half in range(2):
+                    bank = tr_pool.tile([P, BANK], F32, name="bank", tag="tr")
                     for a in range(2):
                         for u in range(2):
-                            col = (2 * pair + a) * 512 + 256 * g + 128 * u
+                            first = (2 * half + a) * (K // 2) + 256 * s + P * u
                             nc.tensor.transpose(bank[:, (2 * a + u) * P:(2 * a + u + 1) * P],
-                                                words[:, col:col + P], ident[:])
+                                                words[:, first:first + P], ident[:])
                     banks.append(bank)
             for q in range(4):
-                dst = g32[:, q * 512:(q + 1) * 512].rearrange("p (a r u) -> p a r u", a=2, u=2)
-                src = banks[q][:].rearrange("p (a u r) -> p a r u", a=2, u=2)
-                if q in vector_banks:
-                    nc.vector.tensor_copy(out=dst, in_=src)
-                else:
-                    nc.scalar.copy(out=dst, in_=src)
-            state["raw_live"] -= 1
+                nc.scalar.copy(
+                    out=grouped_words[:, q * BANK:(q + 1) * BANK].rearrange("p (a r u) -> p a r u", a=2, u=2),
+                    in_=banks[q][:].rearrange("p (a u r) -> p a r u", a=2, u=2))
+            progress["waiting"] -= 1
             issue_loads()
 
         def quantise(key):
             if key == "x" or key == "h":
                 m = 0 if key == "x" else 1
-                cd, sc = acodes[m], ascales[m]
+                codes[key] = (act_codes[m], act_scales[m])
             else:
-                cd = wqp.tile([P, 1024], U32, name="wcodes", tag="wcodes", align_bytes=64)
-                sc = wqp.tile([P, 1024], U8, name="wscales", tag="wscales", align_bytes=64)
-            nc.vector.quantize_mx(out=cd[:].bitcast(FP8X4), scales=sc[:], in_=grouped[key][:])
-            codes[key] = (cd, sc)
+                codes[key] = (weight_pool.tile([P, 2 * BANK], U32, name="w_codes", tag="w_codes", align_bytes=64),
+                              weight_pool.tile([P, 2 * BANK], U8, name="w_scales", tag="w_scales", align_bytes=64))
+            nc.vector.quantize_mx(out=codes[key][0][:].bitcast(FP8X4), scales=codes[key][1][:],
+                                  in_=grouped[key][:])
 
-        zbanks = {}
+        z_banks = {}
 
-        def open_banks(c):
-            zbanks[c] = [zp.tile([P, 512], F32, name="z%d" % bb, tag="z") for bb in range(4)]
+        def mx_passes(c, m):
+            if m == 0:
+                z_banks[c] = [z_pool.tile([P, BANK], F32, name="z%d" % j, tag="z") for j in range(SLABS)]
+            w_codes, w_scales = codes["w%d" % (2 * c + m)]
+            for j in range(SLABS):
+                for s in range(2):
+                    rows = slice(s * BANK + j * P, s * BANK + (j + 1) * P)
+                    cols = slice(s * BANK, (s + 1) * BANK)
+                    nc.tensor.matmul_mx(out=z_banks[c][j][:],
+                                        lhsT=act_codes[m][:, rows].bitcast(FP8X4), lhsT_scale=act_scales[m][:, rows],
+                                        rhs=w_codes[:, cols].bitcast(FP8X4), rhs_scale=w_scales[:, cols],
+                                        start=(m == 0 and s == 0), stop=(m == 1 and s == 1))
 
-        def mx_passes(c, bb, m):
-            cd, sc = codes["w%d" % (2 * c + m)]
-            for g in range(2):
-                a0 = g * 512 + bb * P
-                nc.tensor.matmul_mx(out=zbanks[c][bb][:],
-                                    lhsT=acodes[m][:, a0:a0 + P].bitcast(FP8X4),
-                                    lhsT_scale=ascales[m][:, a0:a0 + P],
-                                    rhs=cd[:, g * 512:(g + 1) * 512].bitcast(FP8X4),
-                                    rhs_scale=sc[:, g * 512:(g + 1) * 512],
-                                    start=(m == 0 and g == 0), stop=(m == 1 and g == 1))
-
-        def bias_rows(gate):
-            ps = zp.tile([P, 1024], BF16, name="bias_ps", tag="z")
+        def spread_bias(gate):
+            spread = z_pool.tile([P, K], BF16, name="spread", tag="z")
             for half in range(2):
-                nc.tensor.matmul(ps[:, half * 512:(half + 1) * 512], lhsT=ones[:],
-                                 rhs=bz[:, gate * 1024 + half * 512:gate * 1024 + (half + 1) * 512],
+                nc.tensor.matmul(spread[:, half * BANK:(half + 1) * BANK], lhsT=ones[:],
+                                 rhs=bias_row[:, gate * K + half * BANK:gate * K + (half + 1) * BANK],
                                  start=True, stop=True)
-            nc.vector.tensor_copy(out=bt[:].rearrange("p (c g r) -> p c g r", c=CHUNKS, g=4)[:, :, gate, :],
-                                  in_=ps[:].rearrange("p (c r) -> p c r", c=CHUNKS))
+            nc.vector.tensor_copy(
+                out=bias_all[:].rearrange("p (c g r) -> p c g r", c=CHUNKS, g=SLABS)[:, :, gate, :],
+                in_=spread[:].rearrange("p (c r) -> p c r", c=CHUNKS))
 
-        acts = {}
+        sums = {}
 
-        def bias_add(c, bb):
-            if bb == 0:
-                acts[c] = app.tile([P, 4, 512], F32, name="a_t", tag="a")
-            nc.vector.tensor_tensor(out=acts[c][:, bb, :], in0=zbanks[c][bb][:],
-                                    in1=bt[:, c * 512:(c + 1) * 512], op=ALU.add)
+        def add_bias(c, j):
+            if j == 0:
+                sums[c] = sums_pool.tile([P, SLABS, BANK], F32, name="sums", tag="sums")
+            nc.vector.tensor_tensor(out=sums[c][:, j, :], in0=z_banks[c][j][:],
+                                    in1=bias_all[:, c * BANK:(c + 1) * BANK], op=ALU.add)
 
-        def relu(c, b0, b1):
-            a_t = acts[c]
-            nc.scalar.activation(out=a_t[:, b0:b1, 0:384], in_=a_t[:, b0:b1, 0:384], func=ACT.Relu,
-                                 bias=0.5, scale=1.0 / 6.0)
+        def lower_clip(c, j0, j1):
+            view = sums[c][:, j0:j1, 0:3 * P]
+            nc.scalar.activation(out=view, in_=view, func=ACT.Relu, bias=0.5, scale=1.0 / 6.0)
 
-        outs = {}
+        results = {}
 
-        def gate_chain(c, b0, b1):
-            a_t = acts[c]
-            group = [gr for gr in STORE_GROUPS if c in gr][0]
+        def gate_chain(c, j0, j1):
+            group = [members for members in STORE_GROUPS if c in members][0]
             width = P * len(group)
-            if c == group[0] and b0 == 0:
-                outs[group] = (outp.tile([P, 4, width], F32, name="h1_t", tag="h1_%d" % width),
-                               outp.tile([P, 4, width], F32, name="c1_t", tag="c1_%d" % width))
-            h1_t, c1_t = outs[group]
-            lo = (c - group[0]) * P
-            col = group[0] * P
-            old = tmp.tile([P, 4, P], F32, name="old")
-            new = tmp.tile([P, 4, P], F32, name="new")
-            gcl = tmp.tile([P, 4, P], F32, name="gcl")
-            tcl = tmp.tile([P, 4, P], F32, name="tcl")
-            clipper = nc.gpsimd if c + 1 < CHUNKS else nc.vector
+            if c == group[0] and j0 == 0:
+                results[group] = [out_pool.tile([P, SLABS, width], F32, name=n, tag="%s_%d" % (n, width))
+                                  for n in ("h1", "c1")]
+            h1, c1 = [res[:, j0:j1, (c - group[0]) * P:(c - group[0] + 1) * P] for res in results[group]]
+            f, i, o, g = [sums[c][:, j0:j1, n * P:(n + 1) * P] for n in range(4)]
+            old, new, g_clip, c_clip = [gate_pool.tile([P, SLABS, P], F32, name=n)[:, j0:j1, :]
+                                        for n in ("old", "new", "g_clip", "c_clip")]
 
-            def s_gcl():
-                clipper.tensor_scalar(out=gcl[:, b0:b1, :], in0=a_t[:, b0:b1, 384:512], scalar1=-1.0, scalar2=1.0,
-                                        op0=ALU.max, op1=ALU.min)
-
-            def s_old():
-                nc.vector.scalar_tensor_tensor(out=old[:, b0:b1, :], in0=a_t[:, b0:b1, 0:128], scalar=1.0,
-                                               in1=c0[:, b0:b1, c * P:(c + 1) * P], op0=ALU.min, op1=ALU.mult)
-
-            def s_new():
-                nc.vector.scalar_tensor_tensor(out=new[:, b0:b1, :], in0=a_t[:, b0:b1, 128:256], scalar=1.0,
-                                               in1=gcl[:, b0:b1, :], op0=ALU.min, op1=ALU.mult)
-
-            def s_c1():
-                nc.vector.tensor_tensor(out=c1_t[:, b0:b1, lo:lo + P], in0=old[:, b0:b1, :], in1=new[:, b0:b1, :],
-                                     op=ALU.add)
+            def store(n):
                 if c == group[-1]:
-                    nc.sync.dma_start(out=o_views[1][:, b0:b1, col:col + width], in_=c1_t[:, b0:b1, :])
+                    nc.sync.dma_start(out=out_views[n][:, j0:j1, group[0] * P:group[0] * P + width],
+                                      in_=results[group][n][:, j0:j1, :])
 
-            def s_tcl():
-                clipper.tensor_scalar(out=tcl[:, b0:b1, :], in0=c1_t[:, b0:b1, lo:lo + P], scalar1=-1.0, scalar2=1.0,
-                                     op0=ALU.max, op1=ALU.min)
+            def step_g_clip():
+                nc.vector.tensor_scalar(out=g_clip, in0=g, scalar1=-1.0, scalar2=1.0, op0=ALU.max, op1=ALU.min)
 
-            def s_h1():
-                nc.vector.scalar_tensor_tensor(out=h1_t[:, b0:b1, lo:lo + P], in0=a_t[:, b0:b1, 256:384], scalar=1.0,
-                                               in1=tcl[:, b0:b1, :], op0=ALU.min, op1=ALU.mult)
-                if c == group[-1]:
-                    nc.sync.dma_start(out=o_views[0][:, b0:b1, col:col + width], in_=h1_t[:, b0:b1, :])
+            def step_old():
+                nc.vector.scalar_tensor_tensor(out=old, in0=f, scalar=1.0, in1=c0_sb[:, j0:j1, c * P:(c + 1) * P],
+                                               op0=ALU.min, op1=ALU.mult)
 
-            return [s_gcl, s_old, s_new, s_c1, s_tcl, s_h1]
+            def step_new():
+                nc.vector.scalar_tensor_tensor(out=new, in0=i, scalar=1.0, in1=g_clip, op0=ALU.min, op1=ALU.mult)
+
+            def step_c1():
+                nc.vector.tensor_tensor(out=c1, in0=old, in1=new, op=ALU.add)
+                store(1)
+
+            def step_c_clip():
+                nc.vector.tensor_scalar(out=c_clip, in0=c1, scalar1=-1.0, scalar2=1.0, op0=ALU.max, op1=ALU.min)
+
+            def step_h1():
+                nc.vector.scalar_tensor_tensor(out=h1, in0=o, scalar=1.0, in1=c_clip, op0=ALU.min, op1=ALU.mult)
+                store(0)
+
+            return [step_g_clip, step_old, step_new, step_c1, step_c_clip, step_h1]
 
         def alternate(first, second):
-            for i in range(max(len(first), len(second))):
+            for n in range(max(len(first), len(second))):
                 for calls in (first, second):
-                    if i < len(calls):
-                        calls[i]()
+                    if n < len(calls):
+                        calls[n]()
 
-        nc.vector.memset(bz[:].bitcast(I32), 0)
+        nc.vector.memset(bias_row[:].bitcast(I32), 0)
         nc.vector.memset(ones[:], 1.0)
         nc.vector.memset(warm[:], 0.0)
         make_identity(nc, ident[:])
@@ -210,52 +202,45 @@ def tile_qlstmcell_kernel(tc, input_, h_0, c_0, W_ih, W_hh, b_hh, out_0, out_1):
         issue_loads()
 
         transposes("x")
-        bias_rows(0)
-        bias_rows(1)
+        spread_bias(0)
+        spread_bias(1)
         transposes("w0")
         quantise("x")
-        bias_rows(2)
-        bias_rows(3)
+        spread_bias(2)
+        spread_bias(3)
         transposes("h")
         quantise("w0")
         transposes("w1")
-        open_banks(0)
-        for bb in range(4):
-            mx_passes(0, bb, 0)
+        mx_passes(0, 0)
         quantise("h")
         transposes("w2")
         quantise("w1")
         transposes("w3")
         quantise("w2")
-        for bb in range(4):
-            mx_passes(0, bb, 1)
-        for bb in range(4):
-            bias_add(0, bb)
+        mx_passes(0, 1)
+        for j in range(SLABS):
+            add_bias(0, j)
+
         for c in range(1, CHUNKS):
-            if c + 1 < CHUNKS:
+            more = c + 1 < CHUNKS
+            if more:
                 transposes("w%d" % (2 * c + 2))
-            relu(c - 1, 0, 2)
-            relu(c - 1, 2, 4)
-            chain = gate_chain(c - 1, 0, 4)
+            lower_clip(c - 1, 0, SLABS)
+            chain = gate_chain(c - 1, 0, SLABS)
             quantise("w%d" % (2 * c + 1))
-            open_banks(c)
-            for bb in range(4):
-                mx_passes(c, bb, 0)
-            for call in chain[0:3]:
-                call()
-            if c + 1 < CHUNKS:
-                transposes("w%d" % (2 * c + 3))
+            mx_passes(c, 0)
+            chain[0]()
+            if more:
                 quantise("w%d" % (2 * c + 2))
-            for bb in range(4):
-                mx_passes(c, bb, 1)
-            adds = [lambda bb=bb: bias_add(c, bb) for bb in range(4)]
-            if GPSIMD_HELPS:
-                alternate(chain[3:5], [])
-                alternate(adds, [])
-                chain[5]()
-            else:
-                alternate(chain[3:6], adds)
+            chain[1]()
+            chain[2]()
+            if more:
+                transposes("w%d" % (2 * c + 3))
+            mx_passes(c, 1)
+            add_bias(c, 0)
+            alternate([lambda j=j: add_bias(c, j) for j in range(1, SLABS)], chain[3:6])
+
         last = CHUNKS - 1
-        relu(last, 0, 2)
-        relu(last, 2, 4)
+        lower_clip(last, 0, 2)
+        lower_clip(last, 2, 4)
         alternate(gate_chain(last, 0, 2), gate_chain(last, 2, 4))

@@ -176,7 +176,8 @@ def tile_qlstmcell_kernel(tc, input_, h_0, c_0, W_ih, W_hh, b_hh, out_0, out_1):
                 nc.vector.scalar_tensor_tensor(out=new, in0=i, scalar=1.0, in1=g_clip, op0=ALU.min, op1=ALU.mult)
 
             def step_c1():
-                nc.vector.tensor_tensor(out=c1, in0=old, in1=new, op=ALU.add)
+                adder = nc.gpsimd if c + 1 < CHUNKS else nc.vector
+                adder.tensor_tensor(out=c1, in0=old, in1=new, op=ALU.add)
                 store(1)
 
             def step_c_clip():

@@ -212,36 +212,31 @@ def tile_qlstmcell_kernel(tc, input_, h_0, c_0, W_ih, W_hh, b_hh, out_0, out_1):
         transposes("h")
         quantise("w0")
         transposes("w1")
-        mx_passes(0, 0)
         quantise("h")
-        transposes("w2")
-        quantise("w1")
-        transposes("w3")
-        quantise("w2")
-        mx_passes(0, 1)
-        for j in range(SLABS):
-            add_bias(0, j)
 
-        for c in range(1, CHUNKS):
+        for c in range(CHUNKS):
             more = c + 1 < CHUNKS
-            if more:
-                transposes("w%d" % (2 * c + 2))
-            lower_clip(c - 1, 0, SLABS)
-            chain = gate_chain(c - 1, 0, SLABS)
+            chain = []
+            if c > 0:
+                lower_clip(c - 1, 2, 4)
+                chain = gate_chain(c - 1, 0, SLABS)
+            for step in chain[0:1]:
+                step()
             quantise("w%d" % (2 * c + 1))
             mx_passes(c, 0)
-            chain[0]()
             if more:
-                quantise("w%d" % (2 * c + 2))
-            chain[1]()
-            chain[2]()
-            if more:
-                transposes("w%d" % (2 * c + 3))
+                transposes("w%d" % (2 * c + 2))
+            for step in chain[1:4]:
+                step()
             mx_passes(c, 1)
             add_bias(c, 0)
-            alternate([lambda j=j: add_bias(c, j) for j in range(1, SLABS)], chain[3:6])
+            add_bias(c, 1)
+            lower_clip(c, 0, 2)
+            if more:
+                quantise("w%d" % (2 * c + 2))
+                transposes("w%d" % (2 * c + 3))
+            alternate([lambda j=j: add_bias(c, j) for j in range(2, SLABS)], chain[4:6])
 
         last = CHUNKS - 1
-        lower_clip(last, 0, 2)
         lower_clip(last, 2, 4)
         alternate(gate_chain(last, 0, 2), gate_chain(last, 2, 4))

@@ -21,6 +21,7 @@ BANK = 512
 CHUNKS = 8
 RAW_BUFS = 10
 STORE_GROUPS = ((0, 1), (2, 3), (4, 5), (6,), (7,))
+WARM_UP_MATMULS = 7
 
 
 def tile_qlstmcell_kernel(tc, input_, h_0, c_0, W_ih, W_hh, b_hh, out_0, out_1):
@@ -40,11 +41,12 @@ def tile_qlstmcell_kernel(tc, input_, h_0, c_0, W_ih, W_hh, b_hh, out_0, out_1):
         ident = const.tile([P, P], F32, name="ident")
         ones = const.tile([P, P], BF16, name="ones")
         warm = const.tile([P, 8], F32, name="warm")
+        ones_wide = const.tile([P, BANK], BF16, name="ones_wide")
         bias_row = const.tile([P, SLABS * K], BF16, name="bias_row")
         bias_all = const.tile([P, CHUNKS * BANK], BF16, name="bias_all")
         c0_sb = const.tile([P, SLABS, K], BF16, name="c0_sb")
-        act_codes = [const.tile([P, 2 * BANK], U32, name="act_codes%d" % m, align_bytes=64) for m in range(2)]
-        act_scales = [const.tile([P, 2 * BANK], U8, name="act_scales%d" % m, align_bytes=64) for m in range(2)]
+        act_codes = [const.tile([P, 2 * BANK], U32, name="act_codes%d" % m, align_bytes=256) for m in range(2)]
+        act_scales = [const.tile([P, 2 * BANK], U8, name="act_scales%d" % m, align_bytes=256) for m in range(2)]
 
         weight_views = [w.rearrange("(g c r) k -> c r g k", g=SLABS, c=CHUNKS) for w in (W_ih, W_hh)]
         out_views = [o.rearrange("(p j) h -> p j h", j=SLABS) for o in (out_0, out_1)]
@@ -81,7 +83,7 @@ def tile_qlstmcell_kernel(tc, input_, h_0, c_0, W_ih, W_hh, b_hh, out_0, out_1):
         def transposes(key):
             words = raw[key][:].bitcast(F32)
             grouped[key] = grouped_pool.tile([P, 8 * BANK], BF16, name="grouped_" + key, tag="grouped",
-                                             align_bytes=64)
+                                             align_bytes=256)
             grouped_words = grouped[key][:].bitcast(F32)
             banks = []
             for s in range(2):
@@ -105,8 +107,8 @@ def tile_qlstmcell_kernel(tc, input_, h_0, c_0, W_ih, W_hh, b_hh, out_0, out_1):
                 m = 0 if key == "x" else 1
                 codes[key] = (act_codes[m], act_scales[m])
             else:
-                codes[key] = (weight_pool.tile([P, 2 * BANK], U32, name="w_codes", tag="w_codes", align_bytes=64),
-                              weight_pool.tile([P, 2 * BANK], U8, name="w_scales", tag="w_scales", align_bytes=64))
+                codes[key] = (weight_pool.tile([P, 2 * BANK], U32, name="w_codes", tag="w_codes", align_bytes=256),
+                              weight_pool.tile([P, 2 * BANK], U8, name="w_scales", tag="w_scales", align_bytes=256))
             nc.vector.quantize_mx(out=codes[key][0][:].bitcast(FP8X4), scales=codes[key][1][:],
                                   in_=grouped[key][:])
 
@@ -196,9 +198,13 @@ def tile_qlstmcell_kernel(tc, input_, h_0, c_0, W_ih, W_hh, b_hh, out_0, out_1):
                         calls[n]()
 
         nc.vector.memset(bias_row[:].bitcast(I32), 0)
-        nc.vector.memset(ones[:], 1.0)
+        nc.gpsimd.memset(ones[:], 1.0)
+        nc.gpsimd.memset(ones_wide[:], 1.0)
         nc.vector.memset(warm[:], 0.0)
         make_identity(nc, ident[:])
+        unread = z_pool.tile([P, BANK], F32, name="unread", tag="z")
+        for n in range(WARM_UP_MATMULS):
+            nc.tensor.matmul(unread[:], lhsT=ones[:], rhs=ones_wide[:], start=True, stop=True)
         nc.scalar.activation(out=warm[:], in_=warm[:], func=ACT.Relu, bias=0.5, scale=1.0 / 6.0)
         issue_loads()
 

@@ -220,13 +220,14 @@ def tile_qlstmcell_kernel(tc, input_, h_0, c_0, W_ih, W_hh, b_hh, out_0, out_1):
         transposes("w1")
         quantise("h")
 
+        late_h1 = []
         for c in range(CHUNKS):
             more = c + 1 < CHUNKS
             chain = []
             if c > 0:
                 lower_clip(c - 1, 2, 4)
                 chain = gate_chain(c - 1, 0, SLABS)
-            for step in chain[0:1]:
+            for step in chain[0:1] + late_h1:
                 step()
             quantise("w%d" % (2 * c + 1))
             mx_passes(c, 0)
@@ -241,8 +242,15 @@ def tile_qlstmcell_kernel(tc, input_, h_0, c_0, W_ih, W_hh, b_hh, out_0, out_1):
             if more:
                 quantise("w%d" % (2 * c + 2))
                 transposes("w%d" % (2 * c + 3))
-            alternate([lambda j=j: add_bias(c, j) for j in range(2, SLABS)], chain[4:6])
+            add_bias(c, 2)
+            add_bias(c, 3)
+            for step in chain[4:5]:
+                step()
+            late_h1 = chain[5:6]
 
         last = CHUNKS - 1
         lower_clip(last, 2, 4)
-        alternate(gate_chain(last, 0, 2), gate_chain(last, 2, 4))
+        first_half = gate_chain(last, 0, 2)
+        second_half = gate_chain(last, 2, 4)
+        alternate(first_half[0:1] + second_half[0:1], late_h1)
+        alternate(first_half[1:], second_half[1:])

from contextlib import ExitStack

import concourse.mybir as mybir
from concourse.masks import make_identity

FLOPS = 2 * 512 * 4096 * 2048

BF16 = mybir.dt.bfloat16
F32 = mybir.dt.float32
U32 = mybir.dt.uint32
U8 = mybir.dt.uint8
I32 = mybir.dt.int32
FP8X4 = mybir.dt.float8_e4m3fn_x4
ALU = mybir.AluOpType
ACT = mybir.ActivationFunctionType

P = 128
SLABS = 4
K = 1024
BANK = 512
CHUNKS = 8
RAW_BUFS = 10
STORE_GROUPS = ((0, 1), (2, 3), (4, 5), (6,), (7,))
WARM_UP_MATMULS = 7


def tile_qlstmcell_kernel(tc, input_, h_0, c_0, W_ih, W_hh, b_hh, out_0, out_1):
    nc = tc.nc
    with ExitStack() as ctx:
        ctx.enter_context(tc.manual_schedule())
        const = ctx.enter_context(tc.tile_pool(name="const", bufs=1))
        raw_pool = ctx.enter_context(tc.tile_pool(name="raw_pool", bufs=RAW_BUFS))
        grouped_pool = ctx.enter_context(tc.tile_pool(name="grouped_pool", bufs=3))
        weight_pool = ctx.enter_context(tc.tile_pool(name="weight_pool", bufs=4))
        sums_pool = ctx.enter_context(tc.tile_pool(name="sums_pool", bufs=2))
        gate_pool = ctx.enter_context(tc.tile_pool(name="gate_pool", bufs=2))
        out_pool = ctx.enter_context(tc.tile_pool(name="out_pool", bufs=3))
        tr_pool = ctx.enter_context(tc.psum_pool(name="tr_pool", bufs=4))
        z_pool = ctx.enter_context(tc.psum_pool(name="z_pool", bufs=4))

        ident = const.tile([P, P], F32, name="ident")
        ones = const.tile([P, P], BF16, name="ones")
        warm = const.tile([P, 8], F32, name="warm")
        ones_wide = const.tile([P, BANK], BF16, name="ones_wide")
        bias_row = const.tile([P, SLABS * K], BF16, name="bias_row")
        bias_all = const.tile([P, CHUNKS * BANK], BF16, name="bias_all")
        c0_sb = const.tile([P, SLABS, K], BF16, name="c0_sb")
        act_codes = [const.tile([P, 2 * BANK], U32, name="act_codes%d" % m, align_bytes=256) for m in range(2)]
        act_scales = [const.tile([P, 2 * BANK], U8, name="act_scales%d" % m, align_bytes=256) for m in range(2)]

        weight_views = [w.rearrange("(g c r) k -> c r g k", g=SLABS, c=CHUNKS) for w in (W_ih, W_hh)]
        out_views = [o.rearrange("(p j) h -> p j h", j=SLABS) for o in (out_0, out_1)]

        loads = [("x", input_.rearrange("(p j) k -> p j k", j=SLABS)),
                 ("bias", b_hh.rearrange("(o n) -> o n", o=1)),
                 ("w0", weight_views[0][0]),
                 ("h", h_0.rearrange("(p j) k -> p j k", j=SLABS))]
        for t in range(1, 2 * CHUNKS):
            loads.append(("w%d" % t, weight_views[t % 2][t // 2]))
            if t == 4:
                loads.append(("c0", c_0.rearrange("(p j) h -> p j h", j=SLABS)))
        raw = {}
        progress = {"issued": 0, "waiting": 0}

        def issue_loads():
            while progress["issued"] < len(loads):
                key, view = loads[progress["issued"]]
                if key == "c0":
                    nc.sync.dma_start(out=c0_sb[:], in_=view)
                elif key == "bias":
                    nc.sync.dma_start(out=bias_row[0:1, :], in_=view)
                else:
                    if progress["waiting"] == RAW_BUFS:
                        return
                    raw[key] = raw_pool.tile([P, SLABS * K], BF16, name="raw_" + key, tag="raw")
                    nc.sync.dma_start(out=raw[key][:].rearrange("p (j k) -> p j k", j=SLABS), in_=view)
                    progress["waiting"] += 1
                progress["issued"] += 1

        grouped = {}
        codes = {}

        def transposes(key):
            words = raw[key][:].bitcast(F32)
            grouped[key] = grouped_pool.tile([P, 8 * BANK], BF16, name="grouped_" + key, tag="grouped",
                                             align_bytes=256)
            grouped_words = grouped[key][:].bitcast(F32)
            banks = []
            for s in range(2):
                for half in range(2):
                    bank = tr_pool.tile([P, BANK], F32, name="bank", tag="tr")
                    for a in range(2):
                        for u in range(2):
                            first = (2 * half + a) * (K // 2) + 256 * s + P * u
                            nc.tensor.transpose(bank[:, (2 * a + u) * P:(2 * a + u + 1) * P],
                                                words[:, first:first + P], ident[:])
                    banks.append(bank)
            for q in range(4):
                nc.scalar.copy(
                    out=grouped_words[:, q * BANK:(q + 1) * BANK].rearrange("p (a r u) -> p a r u", a=2, u=2),
                    in_=banks[q][:].rearrange("p (a u r) -> p a r u", a=2, u=2))
            progress["waiting"] -= 1
            issue_loads()

        def quantise(key):
            if key == "x" or key == "h":
                m = 0 if key == "x" else 1
                codes[key] = (act_codes[m], act_scales[m])
            else:
                codes[key] = (weight_pool.tile([P, 2 * BANK], U32, name="w_codes", tag="w_codes", align_bytes=256),
                              weight_pool.tile([P, 2 * BANK], U8, name="w_scales", tag="w_scales", align_bytes=256))
            nc.vector.quantize_mx(out=codes[key][0][:].bitcast(FP8X4), scales=codes[key][1][:],
                                  in_=grouped[key][:])

        z_banks = {}

        def mx_passes(c, m):
            if m == 0:
                z_banks[c] = [z_pool.tile([P, BANK], F32, name="z%d" % j, tag="z") for j in range(SLABS)]
            w_codes, w_scales = codes["w%d" % (2 * c + m)]
            for j in range(SLABS):
                for s in range(2):
                    rows = slice(s * BANK + j * P, s * BANK + (j + 1) * P)
                    cols = slice(s * BANK, (s + 1) * BANK)
                    nc.tensor.matmul_mx(out=z_banks[c][j][:],
                                        lhsT=act_codes[m][:, rows].bitcast(FP8X4), lhsT_scale=act_scales[m][:, rows],
                                        rhs=w_codes[:, cols].bitcast(FP8X4), rhs_scale=w_scales[:, cols],
                                        start=(m == 0 and s == 0), stop=(m == 1 and s == 1))

        def spread_bias(gate):
            spread = z_pool.tile([P, K], BF16, name="spread", tag="z")
            for half in range(2):
                nc.tensor.matmul(spread[:, half * BANK:(half + 1) * BANK], lhsT=ones[:],
                                 rhs=bias_row[:, gate * K + half * BANK:gate * K + (half + 1) * BANK],
                                 start=True, stop=True)
            nc.vector.tensor_copy(
                out=bias_all[:].rearrange("p (c g r) -> p c g r", c=CHUNKS, g=SLABS)[:, :, gate, :],
                in_=spread[:].rearrange("p (c r) -> p c r", c=CHUNKS))

        sums = {}

        def add_bias(c, j):
            if j == 0:
                sums[c] = sums_pool.tile([P, SLABS, BANK], F32, name="sums", tag="sums")
            nc.vector.tensor_tensor(out=sums[c][:, j, :], in0=z_banks[c][j][:],
                                    in1=bias_all[:, c * BANK:(c + 1) * BANK], op=ALU.add)

        def lower_clip(c, j0, j1):
            view = sums[c][:, j0:j1, 0:3 * P]
            nc.scalar.activation(out=view, in_=view, func=ACT.Relu, bias=0.5, scale=1.0 / 6.0)

        results = {}

        def gate_chain(c, j0, j1):
            group = [members for members in STORE_GROUPS if c in members][0]
            width = P * len(group)
            if c == group[0] and j0 == 0:
                results[group] = [out_pool.tile([P, SLABS, width], F32, name=n, tag="%s_%d" % (n, width))
                                  for n in ("h1", "c1")]
            h1, c1 = [res[:, j0:j1, (c - group[0]) * P:(c - group[0] + 1) * P] for res in results[group]]
            f, i, o, g = [sums[c][:, j0:j1, n * P:(n + 1) * P] for n in range(4)]
            old, new, g_clip, c_clip = [gate_pool.tile([P, SLABS, P], F32, name=n)[:, j0:j1, :]
                                        for n in ("old", "new", "g_clip", "c_clip")]

            def store(n):
                if c == group[-1]:
                    nc.sync.dma_start(out=out_views[n][:, j0:j1, group[0] * P:group[0] * P + width],
                                      in_=results[group][n][:, j0:j1, :])

            def step_g_clip():
                nc.vector.tensor_scalar(out=g_clip, in0=g, scalar1=-1.0, scalar2=1.0, op0=ALU.max, op1=ALU.min)

            def step_old():
                nc.vector.scalar_tensor_tensor(out=old, in0=f, scalar=1.0, in1=c0_sb[:, j0:j1, c * P:(c + 1) * P],
                                               op0=ALU.min, op1=ALU.mult)

            def step_new():
                nc.vector.scalar_tensor_tensor(out=new, in0=i, scalar=1.0, in1=g_clip, op0=ALU.min, op1=ALU.mult)

            def step_c1():
                adder = nc.gpsimd if c + 1 < CHUNKS else nc.vector
                adder.tensor_tensor(out=c1, in0=old, in1=new, op=ALU.add)
                store(1)

            def step_c_clip():
                nc.vector.tensor_scalar(out=c_clip, in0=c1, scalar1=-1.0, scalar2=1.0, op0=ALU.max, op1=ALU.min)

            def step_h1():
                nc.vector.scalar_tensor_tensor(out=h1, in0=o, scalar=1.0, in1=c_clip, op0=ALU.min, op1=ALU.mult)
                store(0)

            return [step_g_clip, step_old, step_new, step_c1, step_c_clip, step_h1]

        def alternate(first, second):
            for n in range(max(len(first), len(second))):
                for calls in (first, second):
                    if n < len(calls):
                        calls[n]()

        nc.vector.memset(bias_row[:].bitcast(I32), 0)
        nc.gpsimd.memset(ones[:], 1.0)
        nc.gpsimd.memset(ones_wide[:], 1.0)
        nc.vector.memset(warm[:], 0.0)
        make_identity(nc, ident[:])
        unread = z_pool.tile([P, BANK], F32, name="unread", tag="z")
        for n in range(WARM_UP_MATMULS):
            nc.tensor.matmul(unread[:], lhsT=ones[:], rhs=ones_wide[:], start=True, stop=True)
        nc.scalar.activation(out=warm[:], in_=warm[:], func=ACT.Relu, bias=0.5, scale=1.0 / 6.0)
        issue_loads()

        transposes("x")
        spread_bias(0)
        spread_bias(1)
        transposes("w0")
        quantise("x")
        spread_bias(2)
        spread_bias(3)
        transposes("h")
        quantise("w0")
        transposes("w1")
        quantise("h")

        late_h1 = []
        for c in range(CHUNKS):
            more = c + 1 < CHUNKS
            chain = []
            if c > 0:
                lower_clip(c - 1, 2, 4)
                chain = gate_chain(c - 1, 0, SLABS)
            for step in chain[0:1] + late_h1:
                step()
            quantise("w%d" % (2 * c + 1))
            mx_passes(c, 0)
            if more:
                transposes("w%d" % (2 * c + 2))
            for step in chain[1:4]:
                step()
            mx_passes(c, 1)
            add_bias(c, 0)
            add_bias(c, 1)
            lower_clip(c, 0, 2)
            if more:
                quantise("w%d" % (2 * c + 2))
                transposes("w%d" % (2 * c + 3))
            add_bias(c, 2)
            add_bias(c, 3)
            for step in chain[4:5]:
                step()
            late_h1 = chain[5:6]

        last = CHUNKS - 1
        lower_clip(last, 2, 4)
        first_half = gate_chain(last, 0, 2)
        second_half = gate_chain(last, 2, 4)
        alternate(first_half[0:1] + second_half[0:1], late_h1)
        alternate(first_half[1:], second_half[1:])
